import numpy as np
import ml_dtypes


def mxq(x, axis, fmt="e4m3"):
    dtype, down = {"e4m3": (ml_dtypes.float8_e4m3fn, 7), "e5m2": (ml_dtypes.float8_e5m2, 14)}[fmt]
    v = np.moveaxis(np.asarray(x, np.float32).astype(ml_dtypes.bfloat16).astype(np.float64), axis, -1)
    blocks = v.reshape(v.shape[:-1] + (-1, 32))
    amax = np.abs(blocks).max(-1, keepdims=True)
    byte = np.maximum(np.where(amax > 0, np.frexp(amax)[1] - 1 + 127, 0) - down, 1)
    scale = np.exp2(byte - 127.0)
    codes = (blocks / scale).astype(np.float32).astype(dtype).astype(np.float64)
    return np.moveaxis((codes * scale).reshape(v.shape), -1, axis)


WIDE = False


def mx_kscale(k):
    if not WIDE:
        return np.ones(k)
    levels = np.array([18, -18])
    if k % 512:
        return np.exp2(np.random.permutation(np.resize(levels, k // 32))).repeat(32)
    a = np.empty((k // 512, 16))
    for p in range(k // 512):
        a[p, :8] = np.random.permutation(np.resize(levels, 8))
        for g in range(8):
            far = levels[np.abs(levels - a[p, g]) >= 10]
            a[p, g + 8] = far[np.random.randint(len(far))]
    return np.exp2(a.ravel()).repeat(32)


BF16 = ml_dtypes.bfloat16


def bf(x):
    return np.asarray(x, np.float32).astype(BF16)


def f64(x):
    return np.asarray(x).astype(np.float64)


B, S, D_IN, D_OUT, R = 4, 256, 1024, 1024, 128
T = B * S
SCALING = 2.0


def setup_inputs():
    s = mx_kscale(T)
    s = (s / s.min()).reshape(B, S, 1)
    u = mx_kscale(D_OUT)
    x0 = bf(np.random.standard_normal((B, S, D_IN)))
    w0 = bf(np.random.standard_normal((D_OUT, D_IN)) / np.sqrt(D_IN))
    a_w = bf(np.random.standard_normal((R, D_IN)) / np.sqrt(D_IN))
    b_w = bf(np.random.standard_normal((D_OUT, R)) / np.sqrt(R))
    magnitude = bf(np.random.uniform(size=(1, D_OUT)) + 0.5)
    h_lora = bf(np.random.standard_normal((B, S, R)))
    g = bf(4.0 * np.random.standard_normal((B, S, D_OUT)) * np.exp2(np.random.randint(-6, 1, (B, S, 1))) / s * u)
    pre = f64(x0) @ f64(w0).T + SCALING * (f64(h_lora) @ f64(b_w).T)
    w_eff = f64(w0) + SCALING * (f64(b_w) @ f64(a_w))
    weight_norm = np.sqrt((w_eff * w_eff).sum(axis=1))
    return {"x": bf(f64(x0) * s), "weight": bf(f64(w0) / u[:, None]), "a_w": a_w, "b_w": b_w,
            "magnitude": magnitude, "h_lora": h_lora,
            "pre": np.asarray(pre, np.float32), "w_eff": np.asarray(w_eff, np.float32),
            "weight_norm": np.asarray(weight_norm, np.float32), "grad_out": g}


def reference(x, weight, a_w, b_w, magnitude, h_lora, pre, w_eff, weight_norm, grad_out):
    xf = f64(x).reshape(T, D_IN)
    g = f64(grad_out).reshape(T, D_OUT)
    p = f64(pre).reshape(T, D_OUT)
    n = f64(weight_norm)
    m = f64(magnitude).reshape(-1) / n
    dz = g * m
    dx = mxq(dz, 1, "e5m2") @ mxq(f64(weight), 0, "e4m3")
    dw = mxq(dz, 0, "e5m2").T @ mxq(xf, 0, "e4m3")
    c = (g * p).sum(axis=0) * m / (n * n)
    dw = dw - c[:, None] * f64(w_eff)
    return dx.reshape(B, S, D_IN), dw

@@ -1,0 +1,229 @@
+from contextlib import ExitStack
+
+import concourse.mybir as mybir
+from concourse.masks import make_identity
+
+T, D_IN, D_OUT = 1024, 1024, 1024
+FLOPS = 2 * 2 * T * D_IN * D_OUT
+BYTES = 2 * (T * D_IN + D_OUT * D_IN + T * D_OUT + D_OUT) + 4 * (T * D_OUT + D_OUT * D_IN + D_OUT) + 4 * (T * D_IN + D_OUT * D_IN)
+
+F32 = mybir.dt.float32
+BF16 = mybir.dt.bfloat16
+U32 = mybir.dt.uint32
+U8 = mybir.dt.uint8
+E4M3X4 = mybir.dt.float8_e4m3fn_x4
+E5M2X4 = mybir.dt.float8_e5m2_x4
+MULT = mybir.AluOpType.mult
+ADD = mybir.AluOpType.add
+COPY = mybir.ActivationFunctionType.Copy
+
+P = 128
+J = 4
+K = P * J
+H = 512
+
+
+def tile_loralinear_pa_v_kernel(tc, x, weight, a_w, b_w, magnitude, h_lora, pre, w_eff, weight_norm, grad_out, out_0, out_1):
+    nc = tc.nc
+    x_v = x.flatten_outer_dims().rearrange("(g p j) d -> g p j d", p=P, j=J)
+    g_v = grad_out.flatten_outer_dims().rearrange("(g p j) d -> g p j d", p=P, j=J)
+    p_v = pre.flatten_outer_dims().rearrange("(g p j) d -> g p j d", p=P, j=J)
+    w_v = weight.rearrange("(g p j) d -> g p j d", p=P, j=J)
+    we_v = w_eff.rearrange("(b q) d -> b q d", q=P)
+    o0_v = out_0.flatten_outer_dims().rearrange("(g p j) d -> g j p d", p=P, j=J)
+    o1_v = out_1.rearrange("(b q) d -> b q d", q=P)
+
+    with ExitStack() as ctx:
+        sb = ctx.enter_context(tc.tile_pool(name="sb", bufs=1))
+        ps = ctx.enter_context(tc.psum_pool(name="ps", bufs=1))
+
+        ident = sb.tile([P, P], F32, name="ident")
+        make_identity(nc, ident[:])
+
+        norm8 = sb.tile([8, P], F32, name="norm8")
+        mag8 = sb.tile([8, P], BF16, name="mag8")
+        rn8 = sb.tile([8, P], F32, name="rn8")
+        rn28 = sb.tile([8, P], F32, name="rn28")
+        mk = sb.tile([P, 2, P], F32, name="mk")
+        mcol = sb.tile([P, 8], F32, name="mcol")
+        kcol = sb.tile([P, 8], F32, name="kcol")
+        cpart = sb.tile([P, 16], F32, name="cpart")
+        csum = sb.tile([P, 8], F32, name="csum")
+        negc = sb.tile([P, 8], F32, name="negc")
+
+        t_codes = [sb.tile([P, D_OUT], U32, name="t_codes%d" % g, align_bytes=64) for g in range(2)]
+        t_scale = [sb.tile([P, D_OUT], U8, name="t_scale%d" % g, align_bytes=64) for g in range(2)]
+        f_codes = [sb.tile([P, T], U32, name="f_codes%d" % g, align_bytes=64) for g in range(2)]
+        f_scale = [sb.tile([P, T], U8, name="f_scale%d" % g, align_bytes=64) for g in range(2)]
+        w_codes = [sb.tile([P, D_IN], U32, name="w_codes%d" % g, align_bytes=64) for g in range(2)]
+        w_scale = [sb.tile([P, D_IN], U8, name="w_scale%d" % g, align_bytes=64) for g in range(2)]
+        x_codes = [sb.tile([P, D_IN], U32, name="x_codes%d" % g, align_bytes=64) for g in range(2)]
+        x_scale = [sb.tile([P, D_IN], U8, name="x_scale%d" % g, align_bytes=64) for g in range(2)]
+
+        g_raw, w_raw, x_raw, p_raw, we_raw = {}, {}, {}, {}, {}
+        t_il, w_il, x_il, f_il, gp, m_bank = {}, {}, {}, {}, {}, {}
+
+        def load(store, key, view, dtype, tag, bufs):
+            t = sb.tile([P, J, 1024], dtype, name="%s%d" % (tag, key), tag=tag, bufs=bufs)
+            nc.sync.dma_start(out=t[:], in_=view)
+            store[key] = t
+
+        def interleave(engine, store, raw, g, h, name):
+            t = sb.tile([P, H * J], BF16, name="%s%d%d" % (name, g, h), tag="il", bufs=5, align_bytes=64)
+            out = t[:].rearrange("p (d j) -> p d j", j=J)
+            in_ = raw[g][:, :, h * H:(h + 1) * H].rearrange("p j d -> p d j")
+            if engine == "v":
+                nc.vector.tensor_copy(out=out, in_=in_)
+            elif engine == "s":
+                nc.scalar.copy(out=out, in_=in_)
+            else:
+                nc.gpsimd.tensor_scalar(out=out, in0=in_, scalar1=1.0, scalar2=1.0, op0=MULT, op1=MULT)
+            store[g, h] = t
+
+        def quantize(codes, scales, c0, t, fmt):
+            cols = slice(c0, c0 + H)
+            nc.vector.quantize_mx(out=codes[:, cols].bitcast(fmt), scales=scales[:, cols], in_=t[:])
+
+        def make_dz(g, h):
+            t = sb.tile([P, H * J], BF16, name="t_il%d%d" % (g, h), tag="t_il", bufs=4, align_bytes=64)
+            nc.vector.tensor_tensor(out=t[:].rearrange("p (o j) -> p o j", j=J),
+                                    in0=g_raw[g][:, :, h * H:(h + 1) * H].rearrange("p j o -> p o j"),
+                                    in1=m_bank[h][:].unsqueeze(2).to_broadcast([P, H, J]), op=MULT)
+            t_il[g, h] = t
+
+        def transpose_dz(g, h):
+            words = t_il[g, h][:].bitcast(F32)
+            t = sb.tile([P, K * J], BF16, name="f_il%d%d" % (h, g), tag="f_il", bufs=3, align_bytes=64)
+            f_v = t[:].rearrange("q (u e p t) -> q u e p t", u=2, e=2, t=4)
+            for u in range(2):
+                xt = ps.tile([P, J, P], F32, name="xt", tag="xt", bufs=2)
+                for i in range(4):
+                    w0 = 2 * i + u
+                    nc.tensor.transpose(xt[:, i, :], words[:, w0:w0 + 8 * 127 + 1:8], ident[:])
+                nc.scalar.copy(out=f_v[:, u], in_=xt[:].rearrange("q t p -> q (t p)").bitcast(BF16).rearrange("q (t p e) -> q e p t", t=4, e=2))
+            f_il[h, g] = t
+
+        def matmul_0(g):
+            for j in range(J):
+                m_cols = slice(g * K + j * P, g * K + (j + 1) * P)
+                r = sb.tile([P, D_IN], F32, name="r0", tag="r0", bufs=4)
+                for n in range(2):
+                    n_cols = slice(n * H, (n + 1) * H)
+                    acc = ps.tile([P, H], F32, name="acc", tag="acc", bufs=4)
+                    for q in range(2):
+                        nc.tensor.matmul_mx(out=acc[:], lhsT=f_codes[q][:, m_cols].bitcast(E5M2X4), lhsT_scale=f_scale[q][:, m_cols],
+                                            rhs=w_codes[q][:, n_cols].bitcast(E4M3X4), rhs_scale=w_scale[q][:, n_cols],
+                                            start=(q == 0), stop=(q == 1))
+                    nc.scalar.copy(out=r[:, n_cols], in_=acc[:])
+                nc.sync.dma_start(out=o0_v[g, j], in_=r[:])
+
+        def make_gp(g, h):
+            cols = slice(h * H, (h + 1) * H)
+            t = sb.tile([P, J, H], F32, name="gp%d%d" % (g, h), tag="gp", bufs=2)
+            nc.vector.tensor_tensor(out=t[:], in0=g_raw[g][:, :, cols], in1=p_raw[g][:, :, cols], op=MULT)
+            gp[g, h] = t
+
+        def sum_gp(g, h):
+            for b in range(4):
+                gt = ps.tile([P, J, P], F32, name="gt", tag="m", bufs=2)
+                for j in range(J):
+                    nc.tensor.transpose(gt[:, j, :], gp[g, h][:, j, b * P:(b + 1) * P], ident[:])
+                junk = sb.tile([P, H], BF16, name="junk", tag="junk", bufs=2)
+                i = g * 8 + h * 4 + b
+                nc.scalar.activation(out=junk[:], in_=gt[:].rearrange("q j p -> q (j p)"), func=COPY, accum_out=cpart[:, i:i + 1])
+
+        def matmul_1(b):
+            h, b4 = divmod(b, 4)
+            m_cols = slice(b * P, (b + 1) * P)
+            for n in range(2):
+                n_cols = slice(n * H, (n + 1) * H)
+                acc = ps.tile([P, H], F32, name="acc", tag="acc", bufs=4)
+                for g in range(2):
+                    nc.tensor.matmul_mx(out=acc[:], lhsT=t_codes[g][:, m_cols].bitcast(E5M2X4), lhsT_scale=t_scale[g][:, m_cols],
+                                        rhs=x_codes[g][:, n_cols].bitcast(E4M3X4), rhs_scale=x_scale[g][:, n_cols],
+                                        start=(g == 0), stop=(g == 1))
+                w = we_raw[b][:, n_cols]
+                nc.vector.scalar_tensor_tensor(out=w, in0=w, scalar=negc[:, b:b + 1], in1=acc[:], op0=MULT, op1=ADD)
+            nc.sync.dma_start(out=o1_v[b], in_=we_raw[b][:])
+
+        with tc.manual_schedule():
+            nc.scalar.dma_start(out=norm8[:], in_=weight_norm.rearrange("(b q) -> b q", q=P))
+            nc.scalar.dma_start(out=mag8[:], in_=magnitude.rearrange("a (b q) -> (a b) q", q=P))
+            load(w_raw, 0, w_v[0], BF16, "raw", 4)
+            load(g_raw, 0, g_v[0], BF16, "g_raw", 2)
+            load(g_raw, 1, g_v[1], BF16, "g_raw", 2)
+            load(w_raw, 1, w_v[1], BF16, "raw", 4)
+            load(p_raw, 0, p_v[0], F32, "p_raw", 2)
+            load(p_raw, 1, p_v[1], F32, "p_raw", 2)
+            load(x_raw, 2, x_v[0], BF16, "raw", 4)
+            load(x_raw, 3, x_v[1], BF16, "raw", 4)
+            x_raw[0], x_raw[1] = x_raw[2], x_raw[3]
+            for b in range(8):
+                t = sb.tile([P, D_IN], F32, name="we%d" % b)
+                nc.sync.dma_start(out=t[:], in_=we_v[b])
+                we_raw[b] = t
+
+            nc.vector.memset(mk[:], 0.0)
+            nc.vector.reciprocal(out=rn8[:], in_=norm8[:])
+            nc.vector.tensor_tensor(out=mk[0:8, 0, :], in0=mag8[:], in1=rn8[:], op=MULT)
+            mt = ps.tile([P, 2, P], F32, name="mt", tag="xt", bufs=2)
+            nc.tensor.transpose(mt[:, 0, :], mk[:, 0, :], ident[:])
+            nc.vector.tensor_copy(out=mcol[:], in_=mt[:, 0, 0:8])
+            for h in range(2):
+                bank = ps.tile([P, H], F32, name="mb%d" % h, tag="m", bufs=2)
+                for b in range(4):
+                    i = h * 4 + b
+                    nc.tensor.transpose(bank[:, b * P:(b + 1) * P], mcol[:, i:i + 1].to_broadcast([P, P]), ident[:])
+                m_bank[h] = bank
+            nc.vector.tensor_tensor(out=rn28[:], in0=rn8[:], in1=rn8[:], op=MULT)
+            nc.vector.tensor_tensor(out=mk[0:8, 1, :], in0=mk[0:8, 0, :], in1=rn28[:], op=MULT)
+            kt = ps.tile([P, 2, P], F32, name="kt", tag="xt", bufs=2)
+            nc.tensor.transpose(kt[:, 0, :], mk[:, 1, :], ident[:])
+
+            interleave("s", w_il, w_raw, 0, 1, "w_il")
+            interleave("v", w_il, w_raw, 0, 0, "w_il")
+            quantize(w_codes[0], w_scale[0], 0, w_il[0, 0], E4M3X4)
+            make_dz(0, 0)
+            transpose_dz(0, 0)
+            nc.vector.tensor_copy(out=kcol[:], in_=kt[:, 0, 0:8])
+            make_dz(0, 1)
+            transpose_dz(0, 1)
+            interleave("g", w_il, w_raw, 1, 0, "w_il")
+            interleave("g", w_il, w_raw, 1, 1, "w_il")
+            quantize(w_codes[0], w_scale[0], H, w_il[0, 1], E4M3X4)
+            make_dz(1, 0)
+            transpose_dz(1, 0)
+            quantize(f_codes[0], f_scale[0], 0, f_il[0, 0], E5M2X4)
+            make_dz(1, 1)
+            transpose_dz(1, 1)
+            quantize(f_codes[1], f_scale[1], 0, f_il[1, 0], E5M2X4)
+            quantize(w_codes[1], w_scale[1], 0, w_il[1, 0], E4M3X4)
+            quantize(t_codes[0], t_scale[0], 0, t_il[0, 0], E5M2X4)
+            quantize(w_codes[1], w_scale[1], H, w_il[1, 1], E4M3X4)
+            matmul_0(0)
+            make_gp(0, 0)
+            sum_gp(0, 0)
+            quantize(f_codes[0], f_scale[0], K, f_il[0, 1], E5M2X4)
+            make_gp(0, 1)
+            sum_gp(0, 1)
+            quantize(f_codes[1], f_scale[1], K, f_il[1, 1], E5M2X4)
+            quantize(t_codes[0], t_scale[0], H, t_il[0, 1], E5M2X4)
+            matmul_0(1)
+            make_gp(1, 0)
+            sum_gp(1, 0)
+            quantize(t_codes[1], t_scale[1], 0, t_il[1, 0], E5M2X4)
+            make_gp(1, 1)
+            sum_gp(1, 1)
+            interleave("v", x_il, x_raw, 0, 0, "x_il")
+            quantize(t_codes[1], t_scale[1], H, t_il[1, 1], E5M2X4)
+            interleave("v", x_il, x_raw, 1, 0, "x_il")
+            quantize(x_codes[0], x_scale[0], 0, x_il[0, 0], E4M3X4)
+            interleave("v", x_il, x_raw, 0, 1, "x_il")
+            quantize(x_codes[1], x_scale[1], 0, x_il[1, 0], E4M3X4)
+            interleave("v", x_il, x_raw, 1, 1, "x_il")
+            quantize(x_codes[0], x_scale[0], H, x_il[0, 1], E4M3X4)
+            nc.vector.tensor_tensor(out=csum[:], in0=cpart[:, 0:8], in1=cpart[:, 8:16], op=ADD)
+            quantize(x_codes[1], x_scale[1], H, x_il[1, 1], E4M3X4)
+            nc.vector.scalar_tensor_tensor(out=negc[:], in0=csum[:], scalar=-1.0, in1=kcol[:], op0=MULT, op1=MULT)
+            for b in range(8):
+                matmul_1(b)

@@ -38,14 +38,14 @@ def tile_loralinear_pa_v_kernel(tc, x, weight, a_w, b_w, magnitude, h_lora, pre,
         ps = ctx.enter_context(tc.psum_pool(name="ps", bufs=1))
 
         ident = sb.tile([P, P], F32, name="ident")
+        ident_b = sb.tile([P, P], BF16, name="ident_b")
         make_identity(nc, ident[:])
-
-        norm8 = sb.tile([8, P], F32, name="norm8")
-        mag8 = sb.tile([8, P], BF16, name="mag8")
-        rn8 = sb.tile([8, P], F32, name="rn8")
-        rn28 = sb.tile([8, P], F32, name="rn28")
-        mk = sb.tile([P, 2, P], F32, name="mk")
+        make_identity(nc, ident_b[:])
+        norm_rows = sb.tile([P, P], F32, name="norm_rows")
+        mag_rows = sb.tile([P, P], BF16, name="mag_rows")
+        rcol = sb.tile([P, 8], F32, name="rcol")
         mcol = sb.tile([P, 8], F32, name="mcol")
+        r2col = sb.tile([P, 8], F32, name="r2col")
         kcol = sb.tile([P, 8], F32, name="kcol")
         cpart = sb.tile([P, 16], F32, name="cpart")
         csum = sb.tile([P, 8], F32, name="csum")
@@ -68,50 +68,47 @@ def tile_loralinear_pa_v_kernel(tc, x, weight, a_w, b_w, magnitude, h_lora, pre,
             nc.sync.dma_start(out=t[:], in_=view)
             store[key] = t
 
-        def interleave(engine, store, raw, g, h, name):
-            t = sb.tile([P, H * J], BF16, name="%s%d%d" % (name, g, h), tag="il", bufs=5, align_bytes=64)
-            out = t[:].rearrange("p (d j) -> p d j", j=J)
-            in_ = raw[g][:, :, h * H:(h + 1) * H].rearrange("p j d -> p d j")
+        def il_tile(store, g, name, tag):
+            store[g] = sb.tile([P, 1024, J], BF16, name="%s%d" % (name, g), tag=tag, bufs=2, align_bytes=64)
+
+        def interleave(engine, store, raw, g, h):
+            cols = slice(h * H, (h + 1) * H)
+            out = store[g][:, cols, :]
+            in_ = raw[g][:, :, cols].rearrange("p j d -> p d j")
             if engine == "v":
                 nc.vector.tensor_copy(out=out, in_=in_)
             elif engine == "s":
                 nc.scalar.copy(out=out, in_=in_)
             else:
                 nc.gpsimd.tensor_scalar(out=out, in0=in_, scalar1=1.0, scalar2=1.0, op0=MULT, op1=MULT)
-            store[g, h] = t
 
-        def quantize(codes, scales, c0, t, fmt):
-            cols = slice(c0, c0 + H)
-            nc.vector.quantize_mx(out=codes[:, cols].bitcast(fmt), scales=scales[:, cols], in_=t[:])
+        def quantize(codes, scales, t, fmt):
+            nc.vector.quantize_mx(out=codes[:].bitcast(fmt), scales=scales[:], in_=t[:].rearrange("p w j -> p (w j)"))
 
         def make_dz(g, h):
-            t = sb.tile([P, H * J], BF16, name="t_il%d%d" % (g, h), tag="t_il", bufs=4, align_bytes=64)
-            nc.vector.tensor_tensor(out=t[:].rearrange("p (o j) -> p o j", j=J),
-                                    in0=g_raw[g][:, :, h * H:(h + 1) * H].rearrange("p j o -> p o j"),
+            cols = slice(h * H, (h + 1) * H)
+            nc.vector.tensor_tensor(out=t_il[g][:, cols, :], in0=g_raw[g][:, :, cols].rearrange("p j o -> p o j"),
                                     in1=m_bank[h][:].unsqueeze(2).to_broadcast([P, H, J]), op=MULT)
-            t_il[g, h] = t
 
         def transpose_dz(g, h):
-            words = t_il[g, h][:].bitcast(F32)
-            t = sb.tile([P, K * J], BF16, name="f_il%d%d" % (h, g), tag="f_il", bufs=3, align_bytes=64)
-            f_v = t[:].rearrange("q (u e p t) -> q u e p t", u=2, e=2, t=4)
+            words = t_il[g][:, h * H:(h + 1) * H, :].rearrange("p o j -> p (o j)").bitcast(F32)
+            f_v = f_il[g][:, h * H:(h + 1) * H, :].rearrange("q (u e p) t -> q u e p t", u=2, e=2)
             for u in range(2):
                 xt = ps.tile([P, J, P], F32, name="xt", tag="xt", bufs=2)
                 for i in range(4):
                     w0 = 2 * i + u
                     nc.tensor.transpose(xt[:, i, :], words[:, w0:w0 + 8 * 127 + 1:8], ident[:])
                 nc.scalar.copy(out=f_v[:, u], in_=xt[:].rearrange("q t p -> q (t p)").bitcast(BF16).rearrange("q (t p e) -> q e p t", t=4, e=2))
-            f_il[h, g] = t
 
         def matmul_0(g):
             for j in range(J):
-                m_cols = slice(g * K + j * P, g * K + (j + 1) * P)
                 r = sb.tile([P, D_IN], F32, name="r0", tag="r0", bufs=4)
                 for n in range(2):
                     n_cols = slice(n * H, (n + 1) * H)
                     acc = ps.tile([P, H], F32, name="acc", tag="acc", bufs=4)
                     for q in range(2):
-                        nc.tensor.matmul_mx(out=acc[:], lhsT=f_codes[q][:, m_cols].bitcast(E5M2X4), lhsT_scale=f_scale[q][:, m_cols],
+                        m_cols = slice(q * H + j * P, q * H + (j + 1) * P)
+                        nc.tensor.matmul_mx(out=acc[:], lhsT=f_codes[g][:, m_cols].bitcast(E5M2X4), lhsT_scale=f_scale[g][:, m_cols],
                                             rhs=w_codes[q][:, n_cols].bitcast(E4M3X4), rhs_scale=w_scale[q][:, n_cols],
                                             start=(q == 0), stop=(q == 1))
                     nc.scalar.copy(out=r[:, n_cols], in_=acc[:])
@@ -119,7 +116,7 @@ def tile_loralinear_pa_v_kernel(tc, x, weight, a_w, b_w, magnitude, h_lora, pre,
 
         def make_gp(g, h):
             cols = slice(h * H, (h + 1) * H)
-            t = sb.tile([P, J, H], F32, name="gp%d%d" % (g, h), tag="gp", bufs=2)
+            t = sb.tile([P, J, H], F32, name="gp%d%d" % (g, h), tag="gp", bufs=3)
             nc.vector.tensor_tensor(out=t[:], in0=g_raw[g][:, :, cols], in1=p_raw[g][:, :, cols], op=MULT)
             gp[g, h] = t
 
@@ -144,86 +141,85 @@ def tile_loralinear_pa_v_kernel(tc, x, weight, a_w, b_w, magnitude, h_lora, pre,
                                         start=(g == 0), stop=(g == 1))
                 w = we_raw[b][:, n_cols]
                 nc.vector.scalar_tensor_tensor(out=w, in0=w, scalar=negc[:, b:b + 1], in1=acc[:], op0=MULT, op1=ADD)
-            nc.sync.dma_start(out=o1_v[b], in_=we_raw[b][:])
+                if b == 7:
+                    nc.sync.dma_start(out=o1_v[b][:, n_cols], in_=w)
+            if b < 7:
+                nc.sync.dma_start(out=o1_v[b], in_=we_raw[b])
+
+        def correction(h):
+            cols = slice(4 * h, 4 * h + 4)
+            nc.vector.tensor_tensor(out=csum[:, cols], in0=cpart[:, cols], in1=cpart[:, 8 + 4 * h:12 + 4 * h], op=ADD)
+            nc.vector.scalar_tensor_tensor(out=negc[:, cols], in0=csum[:, cols], scalar=-1.0, in1=kcol[:, cols], op0=MULT, op1=MULT)
 
         with tc.manual_schedule():
-            nc.scalar.dma_start(out=norm8[:], in_=weight_norm.rearrange("(b q) -> b q", q=P))
-            nc.scalar.dma_start(out=mag8[:], in_=magnitude.rearrange("a (b q) -> (a b) q", q=P))
-            load(w_raw, 0, w_v[0], BF16, "raw", 4)
+            nc.vector.memset(norm_rows[:], 0.0)
+            nc.vector.memset(mag_rows[:], 0.0)
+            nc.scalar.dma_start(out=norm_rows[0:8, :], in_=weight_norm.rearrange("(b q) -> b q", q=P))
+            nc.scalar.dma_start(out=mag_rows[0:8, :], in_=magnitude.rearrange("a (b q) -> (a b) q", q=P))
             load(g_raw, 0, g_v[0], BF16, "g_raw", 2)
+            load(w_raw, 0, w_v[0], BF16, "raw", 3)
             load(g_raw, 1, g_v[1], BF16, "g_raw", 2)
-            load(w_raw, 1, w_v[1], BF16, "raw", 4)
-            load(p_raw, 0, p_v[0], F32, "p_raw", 2)
-            load(p_raw, 1, p_v[1], F32, "p_raw", 2)
-            load(x_raw, 2, x_v[0], BF16, "raw", 4)
-            load(x_raw, 3, x_v[1], BF16, "raw", 4)
+            load(w_raw, 1, w_v[1], BF16, "raw", 3)
+            load(p_raw, 0, p_v[0], F32, "big", 3)
+            load(p_raw, 1, p_v[1], F32, "big", 3)
+            load(x_raw, 2, x_v[0], BF16, "raw", 3)
+            load(x_raw, 3, x_v[1], BF16, "raw", 3)
             x_raw[0], x_raw[1] = x_raw[2], x_raw[3]
-            for b in range(8):
-                t = sb.tile([P, D_IN], F32, name="we%d" % b)
-                nc.sync.dma_start(out=t[:], in_=we_v[b])
-                we_raw[b] = t
+            for h in range(2):
+                t = sb.tile([P, 4, D_IN], F32, name="we%d" % h, tag="big", bufs=3)
+                for b4 in range(4):
+                    b = 4 * h + b4
+                    nc.sync.dma_start(out=t[:, b4, :], in_=we_v[b])
+                    we_raw[b] = t[:, b4, :]
 
-            nc.vector.memset(mk[:], 0.0)
-            nc.vector.reciprocal(out=rn8[:], in_=norm8[:])
-            nc.vector.tensor_tensor(out=mk[0:8, 0, :], in0=mag8[:], in1=rn8[:], op=MULT)
-            mt = ps.tile([P, 2, P], F32, name="mt", tag="xt", bufs=2)
-            nc.tensor.transpose(mt[:, 0, :], mk[:, 0, :], ident[:])
-            nc.vector.tensor_copy(out=mcol[:], in_=mt[:, 0, 0:8])
+            nt = ps.tile([P, P], F32, name="nt", tag="xt", bufs=2)
+            mt = ps.tile([P, P], BF16, name="mt", tag="xt", bufs=2)
+            nc.tensor.transpose(nt[:], norm_rows[:], ident[:])
+            nc.tensor.transpose(mt[:], mag_rows[:], ident_b[:])
+            nc.vector.reciprocal(out=rcol[:], in_=nt[:, 0:8])
+            nc.vector.tensor_tensor(out=mcol[:], in0=mt[:, 0:8], in1=rcol[:], op=MULT)
             for h in range(2):
                 bank = ps.tile([P, H], F32, name="mb%d" % h, tag="m", bufs=2)
                 for b in range(4):
                     i = h * 4 + b
                     nc.tensor.transpose(bank[:, b * P:(b + 1) * P], mcol[:, i:i + 1].to_broadcast([P, P]), ident[:])
                 m_bank[h] = bank
-            nc.vector.tensor_tensor(out=rn28[:], in0=rn8[:], in1=rn8[:], op=MULT)
-            nc.vector.tensor_tensor(out=mk[0:8, 1, :], in0=mk[0:8, 0, :], in1=rn28[:], op=MULT)
-            kt = ps.tile([P, 2, P], F32, name="kt", tag="xt", bufs=2)
-            nc.tensor.transpose(kt[:, 0, :], mk[:, 1, :], ident[:])
 
-            interleave("s", w_il, w_raw, 0, 1, "w_il")
-            interleave("v", w_il, w_raw, 0, 0, "w_il")
-            quantize(w_codes[0], w_scale[0], 0, w_il[0, 0], E4M3X4)
-            make_dz(0, 0)
-            transpose_dz(0, 0)
-            nc.vector.tensor_copy(out=kcol[:], in_=kt[:, 0, 0:8])
-            make_dz(0, 1)
-            transpose_dz(0, 1)
-            interleave("g", w_il, w_raw, 1, 0, "w_il")
-            interleave("g", w_il, w_raw, 1, 1, "w_il")
-            quantize(w_codes[0], w_scale[0], H, w_il[0, 1], E4M3X4)
-            make_dz(1, 0)
-            transpose_dz(1, 0)
-            quantize(f_codes[0], f_scale[0], 0, f_il[0, 0], E5M2X4)
-            make_dz(1, 1)
-            transpose_dz(1, 1)
-            quantize(f_codes[1], f_scale[1], 0, f_il[1, 0], E5M2X4)
-            quantize(w_codes[1], w_scale[1], 0, w_il[1, 0], E4M3X4)
-            quantize(t_codes[0], t_scale[0], 0, t_il[0, 0], E5M2X4)
-            quantize(w_codes[1], w_scale[1], H, w_il[1, 1], E4M3X4)
-            matmul_0(0)
-            make_gp(0, 0)
-            sum_gp(0, 0)
-            quantize(f_codes[0], f_scale[0], K, f_il[0, 1], E5M2X4)
-            make_gp(0, 1)
-            sum_gp(0, 1)
-            quantize(f_codes[1], f_scale[1], K, f_il[1, 1], E5M2X4)
-            quantize(t_codes[0], t_scale[0], H, t_il[0, 1], E5M2X4)
-            matmul_0(1)
-            make_gp(1, 0)
-            sum_gp(1, 0)
-            quantize(t_codes[1], t_scale[1], 0, t_il[1, 0], E5M2X4)
-            make_gp(1, 1)
-            sum_gp(1, 1)
-            interleave("v", x_il, x_raw, 0, 0, "x_il")
-            quantize(t_codes[1], t_scale[1], H, t_il[1, 1], E5M2X4)
-            interleave("v", x_il, x_raw, 1, 0, "x_il")
-            quantize(x_codes[0], x_scale[0], 0, x_il[0, 0], E4M3X4)
-            interleave("v", x_il, x_raw, 0, 1, "x_il")
-            quantize(x_codes[1], x_scale[1], 0, x_il[1, 0], E4M3X4)
-            interleave("v", x_il, x_raw, 1, 1, "x_il")
-            quantize(x_codes[0], x_scale[0], H, x_il[0, 1], E4M3X4)
-            nc.vector.tensor_tensor(out=csum[:], in0=cpart[:, 0:8], in1=cpart[:, 8:16], op=ADD)
-            quantize(x_codes[1], x_scale[1], H, x_il[1, 1], E4M3X4)
-            nc.vector.scalar_tensor_tensor(out=negc[:], in0=csum[:], scalar=-1.0, in1=kcol[:], op0=MULT, op1=MULT)
+            for g in range(2):
+                il_tile(w_il, g, "w_il", "il")
+            interleave("s", w_il, w_raw, 0, 0)
+            interleave("g", w_il, w_raw, 0, 1)
+            interleave("g", w_il, w_raw, 1, 0)
+            interleave("g", w_il, w_raw, 1, 1)
+            for g in range(2):
+                il_tile(t_il, g, "t_il", "t_il")
+                il_tile(f_il, g, "f_il", "f_il")
+                for h in range(2):
+                    make_dz(g, h)
+                    transpose_dz(g, h)
+            nc.vector.tensor_tensor(out=r2col[:], in0=rcol[:], in1=rcol[:], op=MULT)
+            for g in range(2):
+                for h in range(2):
+                    make_gp(g, h)
+                    sum_gp(g, h)
+            nc.vector.tensor_tensor(out=kcol[:], in0=r2col[:], in1=mcol[:], op=MULT)
+            quantize(w_codes[0], w_scale[0], w_il[0], E4M3X4)
+            quantize(f_codes[0], f_scale[0], f_il[0], E5M2X4)
+            quantize(w_codes[1], w_scale[1], w_il[1], E4M3X4)
+            for g in range(2):
+                il_tile(x_il, g, "x_il", "il")
+            interleave("v", x_il, x_raw, 0, 0)
+            quantize(f_codes[1], f_scale[1], f_il[1], E5M2X4)
+            interleave("v", x_il, x_raw, 0, 1)
+            quantize(t_codes[0], t_scale[0], t_il[0], E5M2X4)
+            interleave("v", x_il, x_raw, 1, 0)
+            quantize(x_codes[0], x_scale[0], x_il[0], E4M3X4)
+            interleave("v", x_il, x_raw, 1, 1)
+            quantize(t_codes[1], t_scale[1], t_il[1], E5M2X4)
+            correction(0)
+            quantize(x_codes[1], x_scale[1], x_il[1], E4M3X4)
+            correction(1)
+            for g in range(2):
+                matmul_0(g)
             for b in range(8):
                 matmul_1(b)

@@ -38,11 +38,10 @@ def tile_loralinear_pa_v_kernel(tc, x, weight, a_w, b_w, magnitude, h_lora, pre,
         ps = ctx.enter_context(tc.psum_pool(name="ps", bufs=1))
 
         ident = sb.tile([P, P], F32, name="ident")
-        ident_b = sb.tile([P, P], BF16, name="ident_b")
         make_identity(nc, ident[:])
-        make_identity(nc, ident_b[:])
-        norm_rows = sb.tile([P, P], F32, name="norm_rows")
-        mag_rows = sb.tile([P, P], BF16, name="mag_rows")
+        norm8 = sb.tile([8, P], F32, name="norm8")
+        mag8 = sb.tile([8, P], BF16, name="mag8")
+        rows = sb.tile([P, 2, P], F32, name="rows")
         rcol = sb.tile([P, 8], F32, name="rcol")
         mcol = sb.tile([P, 8], F32, name="mcol")
         r2col = sb.tile([P, 8], F32, name="r2col")
@@ -152,10 +151,9 @@ def tile_loralinear_pa_v_kernel(tc, x, weight, a_w, b_w, magnitude, h_lora, pre,
             nc.vector.scalar_tensor_tensor(out=negc[:, cols], in0=csum[:, cols], scalar=-1.0, in1=kcol[:, cols], op0=MULT, op1=MULT)
 
         with tc.manual_schedule():
-            nc.vector.memset(norm_rows[:], 0.0)
-            nc.vector.memset(mag_rows[:], 0.0)
-            nc.scalar.dma_start(out=norm_rows[0:8, :], in_=weight_norm.rearrange("(b q) -> b q", q=P))
-            nc.scalar.dma_start(out=mag_rows[0:8, :], in_=magnitude.rearrange("a (b q) -> (a b) q", q=P))
+            nc.sync.dma_start(out=norm8[:], in_=weight_norm.rearrange("(b q) -> b q", q=P))
+            nc.scalar.dma_start(out=mag8[:], in_=magnitude.rearrange("a (b q) -> (a b) q", q=P))
+            nc.vector.memset(rows[:], 0.0)
             load(g_raw, 0, g_v[0], BF16, "g_raw", 2)
             load(w_raw, 0, w_v[0], BF16, "raw", 3)
             load(g_raw, 1, g_v[1], BF16, "g_raw", 2)
@@ -172,12 +170,13 @@ def tile_loralinear_pa_v_kernel(tc, x, weight, a_w, b_w, magnitude, h_lora, pre,
                     nc.sync.dma_start(out=t[:, b4, :], in_=we_v[b])
                     we_raw[b] = t[:, b4, :]
 
-            nt = ps.tile([P, P], F32, name="nt", tag="xt", bufs=2)
-            mt = ps.tile([P, P], BF16, name="mt", tag="xt", bufs=2)
-            nc.tensor.transpose(nt[:], norm_rows[:], ident[:])
-            nc.tensor.transpose(mt[:], mag_rows[:], ident_b[:])
-            nc.vector.reciprocal(out=rcol[:], in_=nt[:, 0:8])
-            nc.vector.tensor_tensor(out=mcol[:], in0=mt[:, 0:8], in1=rcol[:], op=MULT)
+            nc.vector.tensor_copy(out=rows[0:8, 0, :], in_=norm8[:])
+            nc.vector.tensor_copy(out=rows[0:8, 1, :], in_=mag8[:])
+            nt = ps.tile([P, 2, P], F32, name="nt", tag="xt", bufs=2)
+            nc.tensor.transpose(nt[:, 0, :], rows[:, 0, :], ident[:])
+            nc.tensor.transpose(nt[:, 1, :], rows[:, 1, :], ident[:])
+            nc.vector.reciprocal(out=rcol[:], in_=nt[:, 0, 0:8])
+            nc.vector.tensor_tensor(out=mcol[:], in0=nt[:, 1, 0:8], in1=rcol[:], op=MULT)
             for h in range(2):
                 bank = ps.tile([P, H], F32, name="mb%d" % h, tag="m", bufs=2)
                 for b in range(4):

@@ -46,6 +46,7 @@ def tile_loralinear_pa_v_kernel(tc, x, weight, a_w, b_w, magnitude, h_lora, pre,
         mcol = sb.tile([P, 8], F32, name="mcol")
         r2col = sb.tile([P, 8], F32, name="r2col")
         kcol = sb.tile([P, 8], F32, name="kcol")
+        kneg = sb.tile([P, 8], F32, name="kneg")
         cpart = sb.tile([P, 16], F32, name="cpart")
         csum = sb.tile([P, 8], F32, name="csum")
         negc = sb.tile([P, 8], F32, name="negc")
@@ -72,8 +73,8 @@ def tile_loralinear_pa_v_kernel(tc, x, weight, a_w, b_w, magnitude, h_lora, pre,
 
         def interleave(engine, store, raw, g, h):
             cols = slice(h * H, (h + 1) * H)
-            out = store[g][:, cols, :]
-            in_ = raw[g][:, :, cols].rearrange("p j d -> p d j")
+            out = store[g][:, cols, :].rearrange("p (c i) j -> p c j i", i=4)
+            in_ = raw[g][:, :, cols].rearrange("p j (c i) -> p c j i", i=4)
             if engine == "v":
                 nc.vector.tensor_copy(out=out, in_=in_)
             elif engine == "s":
@@ -86,8 +87,9 @@ def tile_loralinear_pa_v_kernel(tc, x, weight, a_w, b_w, magnitude, h_lora, pre,
 
         def make_dz(g, h):
             cols = slice(h * H, (h + 1) * H)
-            nc.vector.tensor_tensor(out=t_il[g][:, cols, :], in0=g_raw[g][:, :, cols].rearrange("p j o -> p o j"),
-                                    in1=m_bank[h][:].unsqueeze(2).to_broadcast([P, H, J]), op=MULT)
+            nc.vector.tensor_tensor(out=t_il[g][:, cols, :].rearrange("p (c i) j -> p c j i", i=4),
+                                    in0=g_raw[g][:, :, cols].rearrange("p j (c i) -> p c j i", i=4),
+                                    in1=m_bank[h][:].rearrange("p (c i) -> p c i", i=4).unsqueeze(2).to_broadcast([P, H // 4, J, 4]), op=MULT)
 
         def transpose_dz(g, h):
             words = t_il[g][:, h * H:(h + 1) * H, :].rearrange("p o j -> p (o j)").bitcast(F32)
@@ -121,7 +123,7 @@ def tile_loralinear_pa_v_kernel(tc, x, weight, a_w, b_w, magnitude, h_lora, pre,
 
         def sum_gp(g, h):
             for b in range(4):
-                gt = ps.tile([P, J, P], F32, name="gt", tag="m", bufs=2)
+                gt = ps.tile([P, J, P], F32, name="gt", tag=("m", "xt")[b % 2], bufs=2)
                 for j in range(J):
                     nc.tensor.transpose(gt[:, j, :], gp[g, h][:, j, b * P:(b + 1) * P], ident[:])
                 junk = sb.tile([P, H], BF16, name="junk", tag="junk", bufs=2)
@@ -147,8 +149,8 @@ def tile_loralinear_pa_v_kernel(tc, x, weight, a_w, b_w, magnitude, h_lora, pre,
 
         def correction(h):
             cols = slice(4 * h, 4 * h + 4)
-            nc.vector.tensor_tensor(out=csum[:, cols], in0=cpart[:, cols], in1=cpart[:, 8 + 4 * h:12 + 4 * h], op=ADD)
-            nc.vector.scalar_tensor_tensor(out=negc[:, cols], in0=csum[:, cols], scalar=-1.0, in1=kcol[:, cols], op0=MULT, op1=MULT)
+            nc.gpsimd.tensor_tensor(out=csum[:, cols], in0=cpart[:, cols], in1=cpart[:, 8 + 4 * h:12 + 4 * h], op=ADD)
+            nc.gpsimd.tensor_tensor(out=negc[:, cols], in0=csum[:, cols], in1=kneg[:, cols], op=MULT)
 
         with tc.manual_schedule():
             nc.sync.dma_start(out=norm8[:], in_=weight_norm.rearrange("(b q) -> b q", q=P))
@@ -196,15 +198,18 @@ def tile_loralinear_pa_v_kernel(tc, x, weight, a_w, b_w, magnitude, h_lora, pre,
                 for h in range(2):
                     make_dz(g, h)
                     transpose_dz(g, h)
-            nc.vector.tensor_tensor(out=r2col[:], in0=rcol[:], in1=rcol[:], op=MULT)
-            for g in range(2):
-                for h in range(2):
-                    make_gp(g, h)
-                    sum_gp(g, h)
-            nc.vector.tensor_tensor(out=kcol[:], in0=r2col[:], in1=mcol[:], op=MULT)
+            nc.gpsimd.tensor_tensor(out=r2col[:], in0=rcol[:], in1=rcol[:], op=MULT)
+            nc.gpsimd.tensor_tensor(out=kcol[:], in0=r2col[:], in1=mcol[:], op=MULT)
+            nc.gpsimd.tensor_scalar(out=kneg[:], in0=kcol[:], scalar1=-1.0, scalar2=1.0, op0=MULT, op1=MULT)
+            for g, h in ((0, 0), (0, 1), (1, 0)):
+                make_gp(g, h)
+                sum_gp(g, h)
             quantize(w_codes[0], w_scale[0], w_il[0], E4M3X4)
             quantize(f_codes[0], f_scale[0], f_il[0], E5M2X4)
             quantize(w_codes[1], w_scale[1], w_il[1], E4M3X4)
+            make_gp(1, 1)
+            matmul_0(0)
+            sum_gp(1, 1)
             for g in range(2):
                 il_tile(x_il, g, "x_il", "il")
             interleave("v", x_il, x_raw, 0, 0)
@@ -218,7 +223,6 @@ def tile_loralinear_pa_v_kernel(tc, x, weight, a_w, b_w, magnitude, h_lora, pre,
             correction(0)
             quantize(x_codes[1], x_scale[1], x_il[1], E4M3X4)
             correction(1)
-            for g in range(2):
-                matmul_0(g)
+            matmul_0(1)
             for b in range(8):
                 matmul_1(b)

@@ -80,7 +80,7 @@ def tile_loralinear_pa_v_kernel(tc, x, weight, a_w, b_w, magnitude, h_lora, pre,
             elif engine == "s":
                 nc.scalar.copy(out=out, in_=in_)
             else:
-                nc.gpsimd.tensor_scalar(out=out, in0=in_, scalar1=1.0, scalar2=1.0, op0=MULT, op1=MULT)
+                nc.gpsimd.tensor_scalar(out=store[g][:, cols, :], in0=raw[g][:, :, cols].rearrange("p j d -> p d j"), scalar1=1.0, scalar2=1.0, op0=MULT, op1=MULT)
 
         def quantize(codes, scales, t, fmt):
             nc.vector.quantize_mx(out=codes[:].bitcast(fmt), scales=scales[:], in_=t[:].rearrange("p w j -> p (w j)"))

from contextlib import ExitStack

import concourse.mybir as mybir
from concourse.masks import make_identity

T, D_IN, D_OUT = 1024, 1024, 1024
FLOPS = 2 * 2 * T * D_IN * D_OUT
BYTES = 2 * (T * D_IN + D_OUT * D_IN + T * D_OUT + D_OUT) + 4 * (T * D_OUT + D_OUT * D_IN + D_OUT) + 4 * (T * D_IN + D_OUT * D_IN)

F32 = mybir.dt.float32
BF16 = mybir.dt.bfloat16
U32 = mybir.dt.uint32
U8 = mybir.dt.uint8
E4M3X4 = mybir.dt.float8_e4m3fn_x4
E5M2X4 = mybir.dt.float8_e5m2_x4
MULT = mybir.AluOpType.mult
ADD = mybir.AluOpType.add
COPY = mybir.ActivationFunctionType.Copy

P = 128
J = 4
K = P * J
H = 512


def tile_loralinear_pa_v_kernel(tc, x, weight, a_w, b_w, magnitude, h_lora, pre, w_eff, weight_norm, grad_out, out_0, out_1):
    nc = tc.nc
    x_v = x.flatten_outer_dims().rearrange("(g p j) d -> g p j d", p=P, j=J)
    g_v = grad_out.flatten_outer_dims().rearrange("(g p j) d -> g p j d", p=P, j=J)
    p_v = pre.flatten_outer_dims().rearrange("(g p j) d -> g p j d", p=P, j=J)
    w_v = weight.rearrange("(g p j) d -> g p j d", p=P, j=J)
    we_v = w_eff.rearrange("(b q) d -> b q d", q=P)
    o0_v = out_0.flatten_outer_dims().rearrange("(g p j) d -> g j p d", p=P, j=J)
    o1_v = out_1.rearrange("(b q) d -> b q d", q=P)

    with ExitStack() as ctx:
        sb = ctx.enter_context(tc.tile_pool(name="sb", bufs=1))
        ps = ctx.enter_context(tc.psum_pool(name="ps", bufs=1))

        ident = sb.tile([P, P], F32, name="ident")
        make_identity(nc, ident[:])
        norm8 = sb.tile([8, P], F32, name="norm8")
        mag8 = sb.tile([8, P], BF16, name="mag8")
        rows = sb.tile([P, 2, P], F32, name="rows")
        rcol = sb.tile([P, 8], F32, name="rcol")
        mcol = sb.tile([P, 8], F32, name="mcol")
        r2col = sb.tile([P, 8], F32, name="r2col")
        kcol = sb.tile([P, 8], F32, name="kcol")
        kneg = sb.tile([P, 8], F32, name="kneg")
        cpart = sb.tile([P, 16], F32, name="cpart")
        csum = sb.tile([P, 8], F32, name="csum")
        negc = sb.tile([P, 8], F32, name="negc")

        t_codes = [sb.tile([P, D_OUT], U32, name="t_codes%d" % g, align_bytes=64) for g in range(2)]
        t_scale = [sb.tile([P, D_OUT], U8, name="t_scale%d" % g, align_bytes=64) for g in range(2)]
        f_codes = [sb.tile([P, T], U32, name="f_codes%d" % g, align_bytes=64) for g in range(2)]
        f_scale = [sb.tile([P, T], U8, name="f_scale%d" % g, align_bytes=64) for g in range(2)]
        w_codes = [sb.tile([P, D_IN], U32, name="w_codes%d" % g, align_bytes=64) for g in range(2)]
        w_scale = [sb.tile([P, D_IN], U8, name="w_scale%d" % g, align_bytes=64) for g in range(2)]
        x_codes = [sb.tile([P, D_IN], U32, name="x_codes%d" % g, align_bytes=64) for g in range(2)]
        x_scale = [sb.tile([P, D_IN], U8, name="x_scale%d" % g, align_bytes=64) for g in range(2)]

        g_raw, w_raw, x_raw, p_raw, we_raw = {}, {}, {}, {}, {}
        t_il, w_il, x_il, f_il, gp, m_bank = {}, {}, {}, {}, {}, {}

        def load(store, key, view, dtype, tag, bufs):
            t = sb.tile([P, J, 1024], dtype, name="%s%d" % (tag, key), tag=tag, bufs=bufs)
            nc.sync.dma_start(out=t[:], in_=view)
            store[key] = t

        def il_tile(store, g, name, tag):
            store[g] = sb.tile([P, 1024, J], BF16, name="%s%d" % (name, g), tag=tag, bufs=2, align_bytes=64)

        def interleave(engine, store, raw, g, h):
            cols = slice(h * H, (h + 1) * H)
            out = store[g][:, cols, :].rearrange("p (c i) j -> p c j i", i=4)
            in_ = raw[g][:, :, cols].rearrange("p j (c i) -> p c j i", i=4)
            if engine == "v":
                nc.vector.tensor_copy(out=out, in_=in_)
            elif engine == "s":
                nc.scalar.copy(out=out, in_=in_)
            else:
                nc.gpsimd.tensor_scalar(out=store[g][:, cols, :], in0=raw[g][:, :, cols].rearrange("p j d -> p d j"), scalar1=1.0, scalar2=1.0, op0=MULT, op1=MULT)

        def quantize(codes, scales, t, fmt):
            nc.vector.quantize_mx(out=codes[:].bitcast(fmt), scales=scales[:], in_=t[:].rearrange("p w j -> p (w j)"))

        def make_dz(g, h):
            cols = slice(h * H, (h + 1) * H)
            nc.vector.tensor_tensor(out=t_il[g][:, cols, :].rearrange("p (c i) j -> p c j i", i=4),
                                    in0=g_raw[g][:, :, cols].rearrange("p j (c i) -> p c j i", i=4),
                                    in1=m_bank[h][:].rearrange("p (c i) -> p c i", i=4).unsqueeze(2).to_broadcast([P, H // 4, J, 4]), op=MULT)

        def transpose_dz(g, h):
            words = t_il[g][:, h * H:(h + 1) * H, :].rearrange("p o j -> p (o j)").bitcast(F32)
            f_v = f_il[g][:, h * H:(h + 1) * H, :].rearrange("q (u e p) t -> q u e p t", u=2, e=2)
            for u in range(2):
                xt = ps.tile([P, J, P], F32, name="xt", tag="xt", bufs=2)
                for i in range(4):
                    w0 = 2 * i + u
                    nc.tensor.transpose(xt[:, i, :], words[:, w0:w0 + 8 * 127 + 1:8], ident[:])
                nc.scalar.copy(out=f_v[:, u], in_=xt[:].rearrange("q t p -> q (t p)").bitcast(BF16).rearrange("q (t p e) -> q e p t", t=4, e=2))

        def matmul_0(g):
            for j in range(J):
                r = sb.tile([P, D_IN], F32, name="r0", tag="r0", bufs=4)
                for n in range(2):
                    n_cols = slice(n * H, (n + 1) * H)
                    acc = ps.tile([P, H], F32, name="acc", tag="acc", bufs=4)
                    for q in range(2):
                        m_cols = slice(q * H + j * P, q * H + (j + 1) * P)
                        nc.tensor.matmul_mx(out=acc[:], lhsT=f_codes[g][:, m_cols].bitcast(E5M2X4), lhsT_scale=f_scale[g][:, m_cols],
                                            rhs=w_codes[q][:, n_cols].bitcast(E4M3X4), rhs_scale=w_scale[q][:, n_cols],
                                            start=(q == 0), stop=(q == 1))
                    nc.scalar.copy(out=r[:, n_cols], in_=acc[:])
                nc.sync.dma_start(out=o0_v[g, j], in_=r[:])

        def make_gp(g, h):
            cols = slice(h * H, (h + 1) * H)
            t = sb.tile([P, J, H], F32, name="gp%d%d" % (g, h), tag="gp", bufs=3)
            nc.vector.tensor_tensor(out=t[:], in0=g_raw[g][:, :, cols], in1=p_raw[g][:, :, cols], op=MULT)
            gp[g, h] = t

        def sum_gp(g, h):
            for b in range(4):
                gt = ps.tile([P, J, P], F32, name="gt", tag=("m", "xt")[b % 2], bufs=2)
                for j in range(J):
                    nc.tensor.transpose(gt[:, j, :], gp[g, h][:, j, b * P:(b + 1) * P], ident[:])
                junk = sb.tile([P, H], BF16, name="junk", tag="junk", bufs=2)
                i = g * 8 + h * 4 + b
                nc.scalar.activation(out=junk[:], in_=gt[:].rearrange("q j p -> q (j p)"), func=COPY, accum_out=cpart[:, i:i + 1])

        def matmul_1(b):
            h, b4 = divmod(b, 4)
            m_cols = slice(b * P, (b + 1) * P)
            for n in range(2):
                n_cols = slice(n * H, (n + 1) * H)
                acc = ps.tile([P, H], F32, name="acc", tag="acc", bufs=4)
                for g in range(2):
                    nc.tensor.matmul_mx(out=acc[:], lhsT=t_codes[g][:, m_cols].bitcast(E5M2X4), lhsT_scale=t_scale[g][:, m_cols],
                                        rhs=x_codes[g][:, n_cols].bitcast(E4M3X4), rhs_scale=x_scale[g][:, n_cols],
                                        start=(g == 0), stop=(g == 1))
                w = we_raw[b][:, n_cols]
                nc.vector.scalar_tensor_tensor(out=w, in0=w, scalar=negc[:, b:b + 1], in1=acc[:], op0=MULT, op1=ADD)
                if b == 7:
                    nc.sync.dma_start(out=o1_v[b][:, n_cols], in_=w)
            if b < 7:
                nc.sync.dma_start(out=o1_v[b], in_=we_raw[b])

        def correction(h):
            cols = slice(4 * h, 4 * h + 4)
            nc.gpsimd.tensor_tensor(out=csum[:, cols], in0=cpart[:, cols], in1=cpart[:, 8 + 4 * h:12 + 4 * h], op=ADD)
            nc.gpsimd.tensor_tensor(out=negc[:, cols], in0=csum[:, cols], in1=kneg[:, cols], op=MULT)

        with tc.manual_schedule():
            nc.sync.dma_start(out=norm8[:], in_=weight_norm.rearrange("(b q) -> b q", q=P))
            nc.scalar.dma_start(out=mag8[:], in_=magnitude.rearrange("a (b q) -> (a b) q", q=P))
            nc.vector.memset(rows[:], 0.0)
            load(g_raw, 0, g_v[0], BF16, "g_raw", 2)
            load(w_raw, 0, w_v[0], BF16, "raw", 3)
            load(g_raw, 1, g_v[1], BF16, "g_raw", 2)
            load(w_raw, 1, w_v[1], BF16, "raw", 3)
            load(p_raw, 0, p_v[0], F32, "big", 3)
            load(p_raw, 1, p_v[1], F32, "big", 3)
            load(x_raw, 2, x_v[0], BF16, "raw", 3)
            load(x_raw, 3, x_v[1], BF16, "raw", 3)
            x_raw[0], x_raw[1] = x_raw[2], x_raw[3]
            for h in range(2):
                t = sb.tile([P, 4, D_IN], F32, name="we%d" % h, tag="big", bufs=3)
                for b4 in range(4):
                    b = 4 * h + b4
                    nc.sync.dma_start(out=t[:, b4, :], in_=we_v[b])
                    we_raw[b] = t[:, b4, :]

            nc.vector.tensor_copy(out=rows[0:8, 0, :], in_=norm8[:])
            nc.vector.tensor_copy(out=rows[0:8, 1, :], in_=mag8[:])
            nt = ps.tile([P, 2, P], F32, name="nt", tag="xt", bufs=2)
            nc.tensor.transpose(nt[:, 0, :], rows[:, 0, :], ident[:])
            nc.tensor.transpose(nt[:, 1, :], rows[:, 1, :], ident[:])
            nc.vector.reciprocal(out=rcol[:], in_=nt[:, 0, 0:8])
            nc.vector.tensor_tensor(out=mcol[:], in0=nt[:, 1, 0:8], in1=rcol[:], op=MULT)
            for h in range(2):
                bank = ps.tile([P, H], F32, name="mb%d" % h, tag="m", bufs=2)
                for b in range(4):
                    i = h * 4 + b
                    nc.tensor.transpose(bank[:, b * P:(b + 1) * P], mcol[:, i:i + 1].to_broadcast([P, P]), ident[:])
                m_bank[h] = bank

            for g in range(2):
                il_tile(w_il, g, "w_il", "il")
            interleave("s", w_il, w_raw, 0, 0)
            interleave("g", w_il, w_raw, 0, 1)
            interleave("g", w_il, w_raw, 1, 0)
            interleave("g", w_il, w_raw, 1, 1)
            for g in range(2):
                il_tile(t_il, g, "t_il", "t_il")
                il_tile(f_il, g, "f_il", "f_il")
                for h in range(2):
                    make_dz(g, h)
                    transpose_dz(g, h)
            nc.gpsimd.tensor_tensor(out=r2col[:], in0=rcol[:], in1=rcol[:], op=MULT)
            nc.gpsimd.tensor_tensor(out=kcol[:], in0=r2col[:], in1=mcol[:], op=MULT)
            nc.gpsimd.tensor_scalar(out=kneg[:], in0=kcol[:], scalar1=-1.0, scalar2=1.0, op0=MULT, op1=MULT)
            for g, h in ((0, 0), (0, 1), (1, 0)):
                make_gp(g, h)
                sum_gp(g, h)
            quantize(w_codes[0], w_scale[0], w_il[0], E4M3X4)
            quantize(f_codes[0], f_scale[0], f_il[0], E5M2X4)
            quantize(w_codes[1], w_scale[1], w_il[1], E4M3X4)
            make_gp(1, 1)
            matmul_0(0)
            sum_gp(1, 1)
            for g in range(2):
                il_tile(x_il, g, "x_il", "il")
            interleave("v", x_il, x_raw, 0, 0)
            quantize(f_codes[1], f_scale[1], f_il[1], E5M2X4)
            interleave("v", x_il, x_raw, 0, 1)
            quantize(t_codes[0], t_scale[0], t_il[0], E5M2X4)
            interleave("v", x_il, x_raw, 1, 0)
            quantize(x_codes[0], x_scale[0], x_il[0], E4M3X4)
            interleave("v", x_il, x_raw, 1, 1)
            quantize(t_codes[1], t_scale[1], t_il[1], E5M2X4)
            correction(0)
            quantize(x_codes[1], x_scale[1], x_il[1], E4M3X4)
            correction(1)
            matmul_0(1)
            for b in range(8):
                matmul_1(b)
